import numpy as np
import ml_dtypes


def mxq(x, axis, fmt="e4m3"):
    dtype, down = {"e4m3": (ml_dtypes.float8_e4m3fn, 7), "e5m2": (ml_dtypes.float8_e5m2, 14)}[fmt]
    v = np.moveaxis(np.asarray(x, np.float32).astype(ml_dtypes.bfloat16).astype(np.float64), axis, -1)
    blocks = v.reshape(v.shape[:-1] + (-1, 32))
    amax = np.abs(blocks).max(-1, keepdims=True)
    byte = np.maximum(np.where(amax > 0, np.frexp(amax)[1] - 1 + 127, 0) - down, 1)
    scale = np.exp2(byte - 127.0)
    codes = (blocks / scale).astype(np.float32).astype(dtype).astype(np.float64)
    return np.moveaxis((codes * scale).reshape(v.shape), -1, axis)


WIDE = False


def mx_kscale(k):
    if not WIDE:
        return np.ones(k)
    levels = np.array([10, -10, 5, -5, 0])
    a = np.random.permutation(np.resize(levels, k // 512 * 4)).reshape(k // 512, 4)
    idx = np.arange(k)
    return np.exp2(a[idx // 512, idx % 128 // 32])


BF16 = ml_dtypes.bfloat16


def bf(x):
    return np.asarray(x, np.float32).astype(BF16)


def f64(x):
    return np.asarray(x).astype(np.float64)


B, T, E, Q = 4, 256, 128, 1024
N = B * T


def setup_inputs():
    s = mx_kscale(Q)
    return {"y": bf(np.random.standard_normal((B, T, Q)) * s),
            "w_swiglu": bf(np.random.standard_normal((2 * E, Q)) / np.sqrt(Q) / s)}


def reference(y, w_swiglu):
    uv = mxq(f64(y).reshape(N, Q), 1, "e4m3") @ mxq(f64(w_swiglu).T, 0, "e4m3")
    u, v = uv[:, :E], uv[:, E:]
    ao = mxq(u.T, 1, "e4m3") @ mxq(v, 0, "e4m3")
    return ao / B * E ** (-0.5)

@@ -1,0 +1,145 @@
+from contextlib import ExitStack
+import math
+
+import concourse.mybir as mybir
+from concourse.masks import make_identity
+
+BF16 = mybir.dt.bfloat16
+F32 = mybir.dt.float32
+U32 = mybir.dt.uint32
+U8 = mybir.dt.uint8
+FP8X4 = mybir.dt.float8_e4m3fn_x4
+
+P = 128
+PACK = 4
+K_PASS = P * PACK
+
+BATCH = 4
+TOKENS = 1024
+FEATURES = 1024
+E = 128
+
+FEATURE_PASSES = FEATURES // K_PASS
+TOKEN_PASSES = TOKENS // K_PASS
+TOKEN_TILES = TOKENS // P
+WORDS = FEATURES // 2
+
+TILES_PER_RUN = 2
+
+FLOPS = 2 * TOKENS * FEATURES * 2 * E + 2 * E * E * TOKENS
+
+
+def tile_retentionmechanism_pa_s_kernel(tc, y, w_swiglu, out):
+    nc = tc.nc
+
+    token_tiles = y.flatten_outer_dims().rearrange(
+        "(g p t) q -> g t p q", g=TOKEN_PASSES, p=P, t=PACK
+    )
+    weight_tiles = w_swiglu.rearrange("(a p) q -> a p q", p=P)
+
+    with ExitStack() as ctx:
+        ctx.enter_context(tc.manual_schedule())
+        const = ctx.enter_context(tc.tile_pool(name="const", bufs=1))
+        raw_pool = ctx.enter_context(tc.tile_pool(name="raw", bufs=2 + TOKEN_TILES))
+        grouped_pool = ctx.enter_context(tc.tile_pool(name="grouped", bufs=4))
+        mx_pool = ctx.enter_context(tc.tile_pool(name="mx", bufs=2 + TOKEN_TILES + TOKEN_PASSES))
+        uv_pool = ctx.enter_context(tc.tile_pool(name="uv", bufs=TOKEN_PASSES))
+        flip_psum = ctx.enter_context(tc.psum_pool(name="flip_psum", bufs=4))
+        sums_psum = ctx.enter_context(tc.psum_pool(name="sums_psum", bufs=TOKEN_PASSES))
+
+        def load(rows):
+            raw = raw_pool.tile([P, FEATURES], BF16)
+            nc.sync.dma_start(out=raw[:], in_=rows)
+            return raw
+
+        def flip(raw, copy_out):
+            words = raw[:].bitcast(F32)
+            flipped = flip_psum.tile([P, WORDS], F32)
+            for s in range(WORDS // P):
+                piece = slice(s * P, (s + 1) * P)
+                nc.tensor.transpose(flipped[:, piece], words[:, piece], identity[:])
+            grouped = grouped_pool.tile([P, FEATURES], BF16, align_bytes=64)
+            copy_out(
+                out=grouped[:].bitcast(F32).rearrange("p (c r u) -> p c r u", c=FEATURE_PASSES, u=2),
+                in_=flipped[:].rearrange("p (c u r) -> p c r u", c=FEATURE_PASSES, u=2),
+            )
+            return grouped
+
+        def quantise(grouped, width):
+            codes = mx_pool.tile([P, width // PACK], U32, align_bytes=64)
+            scales = mx_pool.tile([P, width // PACK], U8, align_bytes=64)
+            nc.vector.quantize_mx(out=codes[:].bitcast(FP8X4), scales=scales[:], in_=grouped[:])
+            return codes, scales
+
+        def project(token_mx, sums, t):
+            token_codes, token_scales = token_mx
+            for a in range(2):
+                weight_codes, weight_scales = weight_mx[a]
+                for c in range(FEATURE_PASSES):
+                    cols = slice(c * P, (c + 1) * P)
+                    nc.tensor.matmul_mx(
+                        out=sums[a][:, t * E : (t + 1) * E],
+                        lhsT=token_codes[:, cols].bitcast(FP8X4),
+                        lhsT_scale=token_scales[:, cols],
+                        rhs=weight_codes[:, cols].bitcast(FP8X4),
+                        rhs_scale=weight_scales[:, cols],
+                        start=(c == 0),
+                        stop=(c == FEATURE_PASSES - 1),
+                    )
+
+        identity = const.tile([P, P], F32)
+        make_identity(nc, identity[:])
+
+        weight_raw = [load(weight_tiles[a]) for a in range(2)]
+        token_raw = [load(token_tiles[g, t]) for g in range(TOKEN_PASSES) for t in range(PACK)]
+
+        weight_grouped = [
+            flip(weight_raw[0], nc.scalar.copy),
+            flip(weight_raw[1], nc.vector.tensor_copy),
+        ]
+        weight_mx = [quantise(grouped, FEATURES) for grouped in weight_grouped]
+
+        def flip_run(first):
+            tiles = range(first, first + TILES_PER_RUN)
+            run_grouped = [flip(token_raw[i], nc.scalar.copy) for i in tiles]
+            return [quantise(grouped, FEATURES) for grouped in run_grouped]
+
+        uv_mx = []
+        next_mx = flip_run(0)
+        for first in range(0, TOKEN_TILES, TILES_PER_RUN):
+            run_mx = next_mx
+            if first + TILES_PER_RUN < TOKEN_TILES:
+                next_mx = flip_run(first + TILES_PER_RUN)
+            for j in range(TILES_PER_RUN):
+                t = (first + j) % PACK
+                if t == 0:
+                    u_sums = sums_psum.tile([P, PACK * E], F32)
+                    v_sums = sums_psum.tile([P, PACK * E], F32)
+                project(run_mx[j], (u_sums, v_sums), t)
+                if t == PACK - 1:
+                    uv_grouped = uv_pool.tile([P, 2 * E * PACK], BF16, align_bytes=64)
+                    nc.vector.tensor_copy(
+                        out=uv_grouped[:, : E * PACK].rearrange("p (d t) -> p d t", t=PACK),
+                        in_=u_sums[:].rearrange("p (t d) -> p d t", t=PACK),
+                    )
+                    nc.scalar.copy(
+                        out=uv_grouped[:, E * PACK :].rearrange("p (d t) -> p d t", t=PACK),
+                        in_=v_sums[:].rearrange("p (t d) -> p d t", t=PACK),
+                    )
+                    uv_mx.append(quantise(uv_grouped, 2 * E * PACK))
+
+        out_sums = flip_psum.tile([P, E], F32, tag="flipped")
+        for g in range(TOKEN_PASSES):
+            uv_codes, uv_scales = uv_mx[g]
+            nc.tensor.matmul_mx(
+                out=out_sums[:],
+                lhsT=uv_codes[:, :E].bitcast(FP8X4),
+                lhsT_scale=uv_scales[:, :E],
+                rhs=uv_codes[:, E:].bitcast(FP8X4),
+                rhs_scale=uv_scales[:, E:],
+                start=(g == 0),
+                stop=(g == TOKEN_PASSES - 1),
+            )
+        result = const.tile([P, E], F32)
+        nc.vector.tensor_scalar_mul(out=result[:], in0=out_sums[:], scalar1=1.0 / (BATCH * math.sqrt(E)))
+        nc.sync.dma_start(out=out, in_=result[:])

@@ -26,6 +26,8 @@ WORDS = FEATURES // 2
 
 TILES_PER_RUN = 2
 
+IDLE_MATMULS_AT_START = 4
+
 FLOPS = 2 * TOKENS * FEATURES * 2 * E + 2 * E * E * TOKENS
 
 
@@ -52,12 +54,14 @@ def tile_retentionmechanism_pa_s_kernel(tc, y, w_swiglu, out):
             nc.sync.dma_start(out=raw[:], in_=rows)
             return raw
 
-        def flip(raw, copy_out):
+        def flip(raw, copy_out, before_first_pass):
             words = raw[:].bitcast(F32)
             flipped = flip_psum.tile([P, WORDS], F32)
             for s in range(WORDS // P):
                 piece = slice(s * P, (s + 1) * P)
                 nc.tensor.transpose(flipped[:, piece], words[:, piece], identity[:])
+            if before_first_pass:
+                idle_matmul()
             grouped = grouped_pool.tile([P, FEATURES], BF16, align_bytes=64)
             copy_out(
                 out=grouped[:].bitcast(F32).rearrange("p (c r u) -> p c r u", c=FEATURE_PASSES, u=2),
@@ -87,6 +91,15 @@ def tile_retentionmechanism_pa_s_kernel(tc, y, w_swiglu, out):
                         stop=(c == FEATURE_PASSES - 1),
                     )
 
+        def idle_matmul():
+            nc.tensor.matmul(out=unread[:], lhsT=zeros[:], rhs=zeros[:], start=True, stop=True)
+
+        zeros = const.tile([P, P], F32)
+        nc.vector.memset(zeros[:], 0.0)
+        unread = sums_psum.tile([P, P], F32, tag="u_sums")
+        for n in range(IDLE_MATMULS_AT_START):
+            idle_matmul()
+
         identity = const.tile([P, P], F32)
         make_identity(nc, identity[:])
 
@@ -94,14 +107,14 @@ def tile_retentionmechanism_pa_s_kernel(tc, y, w_swiglu, out):
         token_raw = [load(token_tiles[g, t]) for g in range(TOKEN_PASSES) for t in range(PACK)]
 
         weight_grouped = [
-            flip(weight_raw[0], nc.scalar.copy),
-            flip(weight_raw[1], nc.vector.tensor_copy),
+            flip(weight_raw[0], nc.scalar.copy, True),
+            flip(weight_raw[1], nc.vector.tensor_copy, True),
         ]
         weight_mx = [quantise(grouped, FEATURES) for grouped in weight_grouped]
 
         def flip_run(first):
             tiles = range(first, first + TILES_PER_RUN)
-            run_grouped = [flip(token_raw[i], nc.scalar.copy) for i in tiles]
+            run_grouped = [flip(token_raw[i], nc.scalar.copy, first <= TILES_PER_RUN) for i in tiles]
             return [quantise(grouped, FEATURES) for grouped in run_grouped]
 
         uv_mx = []

@@ -24,9 +24,9 @@ TOKEN_PASSES = TOKENS // K_PASS
 TOKEN_TILES = TOKENS // P
 WORDS = FEATURES // 2
 
-TILES_PER_RUN = 2
+TILES_PER_RUN = 4
 
-IDLE_MATMULS_AT_START = 4
+IDLE_MATMULS_AT_START = 3
 
 FLOPS = 2 * TOKENS * FEATURES * 2 * E + 2 * E * E * TOKENS
 

@@ -26,7 +26,9 @@ WORDS = FEATURES // 2
 
 TILES_PER_RUN = 4
 
-IDLE_MATMULS_AT_START = 3
+IDLE_MATMULS_AT_START = 5
+IDLE_COLUMNS_AT_START = 128
+IDLE_COLUMNS_BEHIND_A_TILE = 64
 
 FLOPS = 2 * TOKENS * FEATURES * 2 * E + 2 * E * E * TOKENS
 
@@ -61,7 +63,7 @@ def tile_retentionmechanism_pa_s_kernel(tc, y, w_swiglu, out):
                 piece = slice(s * P, (s + 1) * P)
                 nc.tensor.transpose(flipped[:, piece], words[:, piece], identity[:])
             if before_first_pass:
-                idle_matmul()
+                idle_matmul(IDLE_COLUMNS_BEHIND_A_TILE)
             grouped = grouped_pool.tile([P, FEATURES], BF16, align_bytes=64)
             copy_out(
                 out=grouped[:].bitcast(F32).rearrange("p (c r u) -> p c r u", c=FEATURE_PASSES, u=2),
@@ -91,14 +93,16 @@ def tile_retentionmechanism_pa_s_kernel(tc, y, w_swiglu, out):
                         stop=(c == FEATURE_PASSES - 1),
                     )
 
-        def idle_matmul():
-            nc.tensor.matmul(out=unread[:], lhsT=zeros[:], rhs=zeros[:], start=True, stop=True)
+        def idle_matmul(columns):
+            nc.tensor.matmul(
+                out=unread[:, :columns], lhsT=zeros[:], rhs=zeros[:, :columns], start=True, stop=True
+            )
 
         zeros = const.tile([P, P], F32)
-        nc.vector.memset(zeros[:], 0.0)
+        nc.gpsimd.memset(zeros[:], 0.0)
         unread = sums_psum.tile([P, P], F32, tag="u_sums")
         for n in range(IDLE_MATMULS_AT_START):
-            idle_matmul()
+            idle_matmul(IDLE_COLUMNS_AT_START)
 
         identity = const.tile([P, P], F32)
         make_identity(nc, identity[:])

@@ -24,7 +24,7 @@ TOKEN_PASSES = TOKENS // K_PASS
 TOKEN_TILES = TOKENS // P
 WORDS = FEATURES // 2
 
-TILES_PER_RUN = 4
+EARLY_TILES = 2
 
 IDLE_MATMULS_AT_START = 5
 IDLE_COLUMNS_AT_START = 128
@@ -46,8 +46,8 @@ def tile_retentionmechanism_pa_s_kernel(tc, y, w_swiglu, out):
         const = ctx.enter_context(tc.tile_pool(name="const", bufs=1))
         raw_pool = ctx.enter_context(tc.tile_pool(name="raw", bufs=2 + TOKEN_TILES))
         grouped_pool = ctx.enter_context(tc.tile_pool(name="grouped", bufs=4))
-        mx_pool = ctx.enter_context(tc.tile_pool(name="mx", bufs=2 + TOKEN_TILES + TOKEN_PASSES))
-        uv_pool = ctx.enter_context(tc.tile_pool(name="uv", bufs=TOKEN_PASSES))
+        mx_pool = ctx.enter_context(tc.tile_pool(name="mx", bufs=2 + TOKEN_TILES + 2 * TOKEN_PASSES))
+        uv_pool = ctx.enter_context(tc.tile_pool(name="uv", bufs=2 * TOKEN_PASSES))
         flip_psum = ctx.enter_context(tc.psum_pool(name="flip_psum", bufs=4))
         sums_psum = ctx.enter_context(tc.psum_pool(name="sums_psum", bufs=TOKEN_PASSES))
 
@@ -77,21 +77,21 @@ def tile_retentionmechanism_pa_s_kernel(tc, y, w_swiglu, out):
             nc.vector.quantize_mx(out=codes[:].bitcast(FP8X4), scales=scales[:], in_=grouped[:])
             return codes, scales
 
-        def project(token_mx, sums, t):
-            token_codes, token_scales = token_mx
-            for a in range(2):
-                weight_codes, weight_scales = weight_mx[a]
-                for c in range(FEATURE_PASSES):
-                    cols = slice(c * P, (c + 1) * P)
-                    nc.tensor.matmul_mx(
-                        out=sums[a][:, t * E : (t + 1) * E],
-                        lhsT=token_codes[:, cols].bitcast(FP8X4),
-                        lhsT_scale=token_scales[:, cols],
-                        rhs=weight_codes[:, cols].bitcast(FP8X4),
-                        rhs_scale=weight_scales[:, cols],
-                        start=(c == 0),
-                        stop=(c == FEATURE_PASSES - 1),
-                    )
+        def project(i, columns):
+            token_codes, token_scales = token_mx[i]
+            weight_codes, weight_scales = weight_mx[columns]
+            g, t = divmod(i, PACK)
+            for c in range(FEATURE_PASSES):
+                cols = slice(c * P, (c + 1) * P)
+                nc.tensor.matmul_mx(
+                    out=uv_sums[g][columns][:, t * E : (t + 1) * E],
+                    lhsT=token_codes[:, cols].bitcast(FP8X4),
+                    lhsT_scale=token_scales[:, cols],
+                    rhs=weight_codes[:, cols].bitcast(FP8X4),
+                    rhs_scale=weight_scales[:, cols],
+                    start=(c == 0),
+                    stop=(c == FEATURE_PASSES - 1),
+                )
 
         def idle_matmul(columns):
             nc.tensor.matmul(
@@ -116,44 +116,53 @@ def tile_retentionmechanism_pa_s_kernel(tc, y, w_swiglu, out):
         ]
         weight_mx = [quantise(grouped, FEATURES) for grouped in weight_grouped]
 
-        def flip_run(first):
-            tiles = range(first, first + TILES_PER_RUN)
-            run_grouped = [flip(token_raw[i], nc.scalar.copy, first <= TILES_PER_RUN) for i in tiles]
-            return [quantise(grouped, FEATURES) for grouped in run_grouped]
+        def round_sums(g, columns, copy_out):
+            rounded = uv_pool.tile([P, E * PACK], BF16, align_bytes=64)
+            copy_out(
+                out=rounded[:].rearrange("p (d t) -> p d t", t=PACK),
+                in_=uv_sums[g][columns][:].rearrange("p (t d) -> p d t", t=PACK),
+            )
+            return rounded
 
-        uv_mx = []
-        next_mx = flip_run(0)
-        for first in range(0, TOKEN_TILES, TILES_PER_RUN):
-            run_mx = next_mx
-            if first + TILES_PER_RUN < TOKEN_TILES:
-                next_mx = flip_run(first + TILES_PER_RUN)
-            for j in range(TILES_PER_RUN):
-                t = (first + j) % PACK
-                if t == 0:
-                    u_sums = sums_psum.tile([P, PACK * E], F32)
-                    v_sums = sums_psum.tile([P, PACK * E], F32)
-                project(run_mx[j], (u_sums, v_sums), t)
-                if t == PACK - 1:
-                    uv_grouped = uv_pool.tile([P, 2 * E * PACK], BF16, align_bytes=64)
-                    nc.vector.tensor_copy(
-                        out=uv_grouped[:, : E * PACK].rearrange("p (d t) -> p d t", t=PACK),
-                        in_=u_sums[:].rearrange("p (t d) -> p d t", t=PACK),
-                    )
-                    nc.scalar.copy(
-                        out=uv_grouped[:, E * PACK :].rearrange("p (d t) -> p d t", t=PACK),
-                        in_=v_sums[:].rearrange("p (t d) -> p d t", t=PACK),
-                    )
-                    uv_mx.append(quantise(uv_grouped, 2 * E * PACK))
+        uv_sums = []
+        for g in range(TOKEN_PASSES):
+            u_sums = sums_psum.tile([P, PACK * E], F32)
+            v_sums = sums_psum.tile([P, PACK * E], F32)
+            uv_sums.append((u_sums, v_sums))
+
+        grouped = [flip(token_raw[i], nc.scalar.copy, True) for i in range(PACK)]
+        token_mx = [quantise(grouped[i], FEATURES) for i in range(PACK)]
+        for i in range(EARLY_TILES):
+            for columns in range(2):
+                project(i, columns)
+
+        grouped = [
+            flip(token_raw[PACK], nc.scalar.copy, False),
+            flip(token_raw[PACK + 1], nc.vector.tensor_copy, False),
+            flip(token_raw[PACK + 2], nc.scalar.copy, False),
+            flip(token_raw[PACK + 3], nc.scalar.copy, False),
+        ]
+        token_mx += [quantise(grouped[t], FEATURES) for t in range(PACK)]
+        for i in range(EARLY_TILES, PACK):
+            for columns in range(2):
+                project(i, columns)
+        rounded = [[round_sums(0, 0, nc.vector.tensor_copy), round_sums(0, 1, nc.scalar.copy)]]
+        uv_mx = [[quantise(part, E * PACK) for part in rounded[0]]]
+        for columns in range(2):
+            for i in range(PACK, TOKEN_TILES):
+                project(i, columns)
+        rounded.append([round_sums(1, columns, nc.scalar.copy) for columns in range(2)])
+        uv_mx.append([quantise(part, E * PACK) for part in rounded[1]])
 
         out_sums = flip_psum.tile([P, E], F32, tag="flipped")
         for g in range(TOKEN_PASSES):
-            uv_codes, uv_scales = uv_mx[g]
+            (u_codes, u_scales), (v_codes, v_scales) = uv_mx[g]
             nc.tensor.matmul_mx(
                 out=out_sums[:],
-                lhsT=uv_codes[:, :E].bitcast(FP8X4),
-                lhsT_scale=uv_scales[:, :E],
-                rhs=uv_codes[:, E:].bitcast(FP8X4),
-                rhs_scale=uv_scales[:, E:],
+                lhsT=u_codes[:].bitcast(FP8X4),
+                lhsT_scale=u_scales[:],
+                rhs=v_codes[:].bitcast(FP8X4),
+                rhs_scale=v_scales[:],
                 start=(g == 0),
                 stop=(g == TOKEN_PASSES - 1),
             )

@@ -28,7 +28,7 @@ EARLY_TILES = 2
 
 IDLE_MATMULS_AT_START = 5
 IDLE_COLUMNS_AT_START = 128
-IDLE_COLUMNS_BEHIND_A_TILE = 64
+IDLE_COLUMNS_BEHIND_A_TILE = 128
 
 FLOPS = 2 * TOKENS * FEATURES * 2 * E + 2 * E * E * TOKENS
 

@@ -26,6 +26,8 @@ WORDS = FEATURES // 2
 
 EARLY_TILES = 2
 
+LOADS = ((0, 0, 2), (0, 2, 2), (1, 0, 2), (1, 2, 1), (1, 3, 1))
+
 IDLE_MATMULS_AT_START = 5
 IDLE_COLUMNS_AT_START = 128
 IDLE_COLUMNS_BEHIND_A_TILE = 128
@@ -36,28 +38,28 @@ FLOPS = 2 * TOKENS * FEATURES * 2 * E + 2 * E * E * TOKENS
 def tile_retentionmechanism_pa_s_kernel(tc, y, w_swiglu, out):
     nc = tc.nc
 
-    token_tiles = y.flatten_outer_dims().rearrange(
-        "(g p t) q -> g t p q", g=TOKEN_PASSES, p=P, t=PACK
+    token_rows = y.flatten_outer_dims().rearrange(
+        "(g p t) q -> g p (t q)", g=TOKEN_PASSES, p=P, t=PACK
     )
     weight_tiles = w_swiglu.rearrange("(a p) q -> a p q", p=P)
 
     with ExitStack() as ctx:
         ctx.enter_context(tc.manual_schedule())
         const = ctx.enter_context(tc.tile_pool(name="const", bufs=1))
-        raw_pool = ctx.enter_context(tc.tile_pool(name="raw", bufs=2 + TOKEN_TILES))
+        raw_pool = ctx.enter_context(tc.tile_pool(name="raw", bufs=1))
         grouped_pool = ctx.enter_context(tc.tile_pool(name="grouped", bufs=4))
         mx_pool = ctx.enter_context(tc.tile_pool(name="mx", bufs=2 + TOKEN_TILES + 2 * TOKEN_PASSES))
         uv_pool = ctx.enter_context(tc.tile_pool(name="uv", bufs=2 * TOKEN_PASSES))
         flip_psum = ctx.enter_context(tc.psum_pool(name="flip_psum", bufs=4))
         sums_psum = ctx.enter_context(tc.psum_pool(name="sums_psum", bufs=TOKEN_PASSES))
 
-        def load(rows):
-            raw = raw_pool.tile([P, FEATURES], BF16)
+        def load(rows, name):
+            raw = raw_pool.tile(list(rows.shape), BF16, name=name)
             nc.sync.dma_start(out=raw[:], in_=rows)
-            return raw
+            return [raw[:, i : i + FEATURES] for i in range(0, rows.shape[1], FEATURES)]
 
         def flip(raw, copy_out, before_first_pass):
-            words = raw[:].bitcast(F32)
+            words = raw.bitcast(F32)
             flipped = flip_psum.tile([P, WORDS], F32)
             for s in range(WORDS // P):
                 piece = slice(s * P, (s + 1) * P)
@@ -107,8 +109,11 @@ def tile_retentionmechanism_pa_s_kernel(tc, y, w_swiglu, out):
         identity = const.tile([P, P], F32)
         make_identity(nc, identity[:])
 
-        weight_raw = [load(weight_tiles[a]) for a in range(2)]
-        token_raw = [load(token_tiles[g, t]) for g in range(TOKEN_PASSES) for t in range(PACK)]
+        weight_raw = [load(weight_tiles[a], "w%d" % a)[0] for a in range(2)]
+        token_raw = []
+        for g, t, count in LOADS:
+            columns = slice(t * FEATURES, (t + count) * FEATURES)
+            token_raw += load(token_rows[g, :, columns], "y%d%d" % (g, t))
 
         weight_grouped = [
             flip(weight_raw[0], nc.scalar.copy, True),

@@ -28,7 +28,7 @@ EARLY_TILES = 2
 
 LOADS = ((0, 0, 2), (0, 2, 2), (1, 0, 2), (1, 2, 1), (1, 3, 1))
 
-IDLE_MATMULS_AT_START = 5
+IDLE_MATMULS_AT_START = 3
 IDLE_COLUMNS_AT_START = 128
 IDLE_COLUMNS_BEHIND_A_TILE = 128
 

@@ -24,7 +24,7 @@ TOKEN_PASSES = TOKENS // K_PASS
 TOKEN_TILES = TOKENS // P
 WORDS = FEATURES // 2
 
-EARLY_TILES = 2
+EARLY_TILES = 0
 
 LOADS = ((0, 0, 2), (0, 2, 2), (1, 0, 2), (1, 2, 1), (1, 3, 1))
 

@@ -24,13 +24,14 @@ TOKEN_PASSES = TOKENS // K_PASS
 TOKEN_TILES = TOKENS // P
 WORDS = FEATURES // 2
 
-EARLY_TILES = 0
+EARLY_TILES = 1
 
 LOADS = ((0, 0, 2), (0, 2, 2), (1, 0, 2), (1, 2, 1), (1, 3, 1))
 
 IDLE_MATMULS_AT_START = 3
 IDLE_COLUMNS_AT_START = 128
 IDLE_COLUMNS_BEHIND_A_TILE = 128
+IDLE_TILES = 2
 
 FLOPS = 2 * TOKENS * FEATURES * 2 * E + 2 * E * E * TOKENS
 
@@ -135,7 +136,7 @@ def tile_retentionmechanism_pa_s_kernel(tc, y, w_swiglu, out):
             v_sums = sums_psum.tile([P, PACK * E], F32)
             uv_sums.append((u_sums, v_sums))
 
-        grouped = [flip(token_raw[i], nc.scalar.copy, True) for i in range(PACK)]
+        grouped = [flip(token_raw[i], nc.scalar.copy, i < IDLE_TILES) for i in range(PACK)]
         token_mx = [quantise(grouped[i], FEATURES) for i in range(PACK)]
         for i in range(EARLY_TILES):
             for columns in range(2):

@@ -24,14 +24,11 @@ TOKEN_PASSES = TOKENS // K_PASS
 TOKEN_TILES = TOKENS // P
 WORDS = FEATURES // 2
 
-EARLY_TILES = 1
-
 LOADS = ((0, 0, 2), (0, 2, 2), (1, 0, 2), (1, 2, 1), (1, 3, 1))
 
 IDLE_MATMULS_AT_START = 3
 IDLE_COLUMNS_AT_START = 128
 IDLE_COLUMNS_BEHIND_A_TILE = 128
-IDLE_TILES = 2
 
 FLOPS = 2 * TOKENS * FEATURES * 2 * E + 2 * E * E * TOKENS
 
@@ -52,20 +49,20 @@ def tile_retentionmechanism_pa_s_kernel(tc, y, w_swiglu, out):
         mx_pool = ctx.enter_context(tc.tile_pool(name="mx", bufs=2 + TOKEN_TILES + 2 * TOKEN_PASSES))
         uv_pool = ctx.enter_context(tc.tile_pool(name="uv", bufs=2 * TOKEN_PASSES))
         flip_psum = ctx.enter_context(tc.psum_pool(name="flip_psum", bufs=4))
-        sums_psum = ctx.enter_context(tc.psum_pool(name="sums_psum", bufs=TOKEN_PASSES))
+        sums_psum = ctx.enter_context(tc.psum_pool(name="sums_psum", bufs=1))
 
         def load(rows, name):
             raw = raw_pool.tile(list(rows.shape), BF16, name=name)
             nc.sync.dma_start(out=raw[:], in_=rows)
             return [raw[:, i : i + FEATURES] for i in range(0, rows.shape[1], FEATURES)]
 
-        def flip(raw, copy_out, before_first_pass):
+        def flip(raw, copy_out, idle):
             words = raw.bitcast(F32)
             flipped = flip_psum.tile([P, WORDS], F32)
-            for s in range(WORDS // P):
-                piece = slice(s * P, (s + 1) * P)
+            for first in range(0, WORDS, P):
+                piece = slice(first, first + P)
                 nc.tensor.transpose(flipped[:, piece], words[:, piece], identity[:])
-            if before_first_pass:
+            if idle:
                 idle_matmul(IDLE_COLUMNS_BEHIND_A_TILE)
             grouped = grouped_pool.tile([P, FEATURES], BF16, align_bytes=64)
             copy_out(
@@ -74,24 +71,27 @@ def tile_retentionmechanism_pa_s_kernel(tc, y, w_swiglu, out):
             )
             return grouped
 
-        def quantise(grouped, width):
-            codes = mx_pool.tile([P, width // PACK], U32, align_bytes=64)
-            scales = mx_pool.tile([P, width // PACK], U8, align_bytes=64)
+        def quantise(grouped):
+            width = grouped.shape[1] // PACK
+            codes = mx_pool.tile([P, width], U32, align_bytes=64)
+            scales = mx_pool.tile([P, width], U8, align_bytes=64)
             nc.vector.quantize_mx(out=codes[:].bitcast(FP8X4), scales=scales[:], in_=grouped[:])
-            return codes, scales
+            return [
+                (codes[:, first : first + P].bitcast(FP8X4), scales[:, first : first + P])
+                for first in range(0, width, P)
+            ]
 
         def project(i, columns):
-            token_codes, token_scales = token_mx[i]
-            weight_codes, weight_scales = weight_mx[columns]
             g, t = divmod(i, PACK)
             for c in range(FEATURE_PASSES):
-                cols = slice(c * P, (c + 1) * P)
+                token_codes, token_scales = token_mx[i][c]
+                weight_codes, weight_scales = weight_mx[columns][c]
                 nc.tensor.matmul_mx(
                     out=uv_sums[g][columns][:, t * E : (t + 1) * E],
-                    lhsT=token_codes[:, cols].bitcast(FP8X4),
-                    lhsT_scale=token_scales[:, cols],
-                    rhs=weight_codes[:, cols].bitcast(FP8X4),
-                    rhs_scale=weight_scales[:, cols],
+                    lhsT=token_codes,
+                    lhsT_scale=token_scales,
+                    rhs=weight_codes,
+                    rhs_scale=weight_scales,
                     start=(c == 0),
                     stop=(c == FEATURE_PASSES - 1),
                 )
@@ -103,7 +103,7 @@ def tile_retentionmechanism_pa_s_kernel(tc, y, w_swiglu, out):
 
         zeros = const.tile([P, P], F32)
         nc.gpsimd.memset(zeros[:], 0.0)
-        unread = sums_psum.tile([P, P], F32, tag="u_sums")
+        unread = sums_psum.tile([P, P], F32, tag="u1")
         for n in range(IDLE_MATMULS_AT_START):
             idle_matmul(IDLE_COLUMNS_AT_START)
 
@@ -116,11 +116,8 @@ def tile_retentionmechanism_pa_s_kernel(tc, y, w_swiglu, out):
             columns = slice(t * FEATURES, (t + count) * FEATURES)
             token_raw += load(token_rows[g, :, columns], "y%d%d" % (g, t))
 
-        weight_grouped = [
-            flip(weight_raw[0], nc.scalar.copy, True),
-            flip(weight_raw[1], nc.vector.tensor_copy, True),
-        ]
-        weight_mx = [quantise(grouped, FEATURES) for grouped in weight_grouped]
+        weight_grouped = [flip(raw, nc.scalar.copy, True) for raw in weight_raw]
+        weight_mx = [quantise(grouped) for grouped in weight_grouped]
 
         def round_sums(g, columns, copy_out):
             rounded = uv_pool.tile([P, E * PACK], BF16, align_bytes=64)
@@ -130,45 +127,55 @@ def tile_retentionmechanism_pa_s_kernel(tc, y, w_swiglu, out):
             )
             return rounded
 
-        uv_sums = []
-        for g in range(TOKEN_PASSES):
-            u_sums = sums_psum.tile([P, PACK * E], F32)
-            v_sums = sums_psum.tile([P, PACK * E], F32)
-            uv_sums.append((u_sums, v_sums))
+        def open_sums(g):
+            return [
+                sums_psum.tile([P, PACK * E], F32, name="%s_sums%d" % (n, g), tag="%s%d" % (n, g))
+                for n in "uv"
+            ]
 
-        grouped = [flip(token_raw[i], nc.scalar.copy, i < IDLE_TILES) for i in range(PACK)]
-        token_mx = [quantise(grouped[i], FEATURES) for i in range(PACK)]
-        for i in range(EARLY_TILES):
-            for columns in range(2):
-                project(i, columns)
+        uv_sums = [open_sums(g) for g in range(TOKEN_PASSES)]
+        grouped = [flip(token_raw[0], nc.scalar.copy, True)]
+        token_mx = [quantise(grouped[0])]
+        grouped += [
+            flip(token_raw[1], nc.vector.tensor_copy, True),
+            flip(token_raw[2], nc.scalar.copy, False),
+            flip(token_raw[3], nc.scalar.copy, False),
+        ]
+        token_mx += [quantise(grouped[i]) for i in range(1, PACK)]
+        project(0, 0)
+        project(0, 1)
 
         grouped = [
-            flip(token_raw[PACK], nc.scalar.copy, False),
-            flip(token_raw[PACK + 1], nc.vector.tensor_copy, False),
-            flip(token_raw[PACK + 2], nc.scalar.copy, False),
-            flip(token_raw[PACK + 3], nc.scalar.copy, False),
+            flip(token_raw[4], nc.scalar.copy, False),
+            flip(token_raw[5], nc.vector.tensor_copy, False),
+            flip(token_raw[6], nc.scalar.copy, False),
+            flip(token_raw[7], nc.scalar.copy, False),
         ]
-        token_mx += [quantise(grouped[t], FEATURES) for t in range(PACK)]
-        for i in range(EARLY_TILES, PACK):
-            for columns in range(2):
-                project(i, columns)
-        rounded = [[round_sums(0, 0, nc.vector.tensor_copy), round_sums(0, 1, nc.scalar.copy)]]
-        uv_mx = [[quantise(part, E * PACK) for part in rounded[0]]]
-        for columns in range(2):
-            for i in range(PACK, TOKEN_TILES):
-                project(i, columns)
-        rounded.append([round_sums(1, columns, nc.scalar.copy) for columns in range(2)])
-        uv_mx.append([quantise(part, E * PACK) for part in rounded[1]])
+        token_mx += [quantise(tile) for tile in grouped]
+        for i in range(1, PACK):
+            project(i, 0)
+            project(i, 1)
+        u_rounded = [round_sums(0, 0, nc.scalar.copy)]
+        v_rounded = [round_sums(0, 1, nc.scalar.copy)]
+        u_mx = quantise(u_rounded[0])
+
+        for i, columns in ((4, 0), (5, 0), (6, 0), (4, 1), (5, 1), (7, 0), (6, 1), (7, 1)):
+            project(i, columns)
+        u_rounded.append(round_sums(1, 0, nc.vector.tensor_copy))
+        v_rounded.append(round_sums(1, 1, nc.scalar.copy))
+        v_mx = quantise(v_rounded[0])
+        u_mx += quantise(u_rounded[1])
+        v_mx += quantise(v_rounded[1])
 
         out_sums = flip_psum.tile([P, E], F32, tag="flipped")
         for g in range(TOKEN_PASSES):
-            (u_codes, u_scales), (v_codes, v_scales) = uv_mx[g]
+            (u_codes, u_scales), (v_codes, v_scales) = u_mx[g], v_mx[g]
             nc.tensor.matmul_mx(
                 out=out_sums[:],
-                lhsT=u_codes[:].bitcast(FP8X4),
-                lhsT_scale=u_scales[:],
-                rhs=v_codes[:].bitcast(FP8X4),
-                rhs_scale=v_scales[:],
+                lhsT=u_codes,
+                lhsT_scale=u_scales,
+                rhs=v_codes,
+                rhs_scale=v_scales,
                 start=(g == 0),
                 stop=(g == TOKEN_PASSES - 1),
             )

@@ -86,8 +86,10 @@ def tile_retentionmechanism_pa_s_kernel(tc, y, w_swiglu, out):
             for c in range(FEATURE_PASSES):
                 token_codes, token_scales = token_mx[i][c]
                 weight_codes, weight_scales = weight_mx[columns][c]
+                banks = uv_sums[g][columns]
+                bank, place = divmod(t, PACK // len(banks))
                 nc.tensor.matmul_mx(
-                    out=uv_sums[g][columns][:, t * E : (t + 1) * E],
+                    out=banks[bank][:, place * E : (place + 1) * E],
                     lhsT=token_codes,
                     lhsT_scale=token_scales,
                     rhs=weight_codes,
@@ -103,7 +105,7 @@ def tile_retentionmechanism_pa_s_kernel(tc, y, w_swiglu, out):
 
         zeros = const.tile([P, P], F32)
         nc.gpsimd.memset(zeros[:], 0.0)
-        unread = sums_psum.tile([P, P], F32, tag="u1")
+        unread = sums_psum.tile([P, P], F32, tag="u1_sums")
         for n in range(IDLE_MATMULS_AT_START):
             idle_matmul(IDLE_COLUMNS_AT_START)
 
@@ -121,24 +123,23 @@ def tile_retentionmechanism_pa_s_kernel(tc, y, w_swiglu, out):
 
         def round_sums(g, columns, copy_out):
             rounded = uv_pool.tile([P, E * PACK], BF16, align_bytes=64)
-            copy_out(
-                out=rounded[:].rearrange("p (d t) -> p d t", t=PACK),
-                in_=uv_sums[g][columns][:].rearrange("p (t d) -> p d t", t=PACK),
-            )
+            by_column = rounded[:].rearrange("p (d t) -> p d t", t=PACK)
+            banks = uv_sums[g][columns]
+            count = PACK // len(banks)
+            for n, bank in enumerate(banks):
+                copy_out(
+                    out=by_column[:, :, n * count : (n + 1) * count],
+                    in_=bank[:].rearrange("p (t d) -> p d t", t=count),
+                )
             return rounded
 
-        def open_sums(g):
-            return [
-                sums_psum.tile([P, PACK * E], F32, name="%s_sums%d" % (n, g), tag="%s%d" % (n, g))
-                for n in "uv"
-            ]
-
-        uv_sums = [open_sums(g) for g in range(TOKEN_PASSES)]
-        grouped = [flip(token_raw[0], nc.scalar.copy, True)]
+        u0_sums = sums_psum.tile([P, PACK * E], F32)
+        v0_sums = sums_psum.tile([P, PACK * E], F32)
+        uv_sums = [([u0_sums], [v0_sums])]
+        grouped = [flip(token_raw[i], nc.scalar.copy, True) for i in range(2)]
         token_mx = [quantise(grouped[0])]
         grouped += [
-            flip(token_raw[1], nc.vector.tensor_copy, True),
-            flip(token_raw[2], nc.scalar.copy, False),
+            flip(token_raw[2], nc.vector.tensor_copy, False),
             flip(token_raw[3], nc.scalar.copy, False),
         ]
         token_mx += [quantise(grouped[i]) for i in range(1, PACK)]
@@ -152,9 +153,13 @@ def tile_retentionmechanism_pa_s_kernel(tc, y, w_swiglu, out):
             flip(token_raw[7], nc.scalar.copy, False),
         ]
         token_mx += [quantise(tile) for tile in grouped]
-        for i in range(1, PACK):
-            project(i, 0)
-            project(i, 1)
+        u1_sums = sums_psum.tile([P, PACK * E], F32)
+        v1_sums = sums_psum.tile([P, PACK * E // 2], F32)
+        v1_last_sums = flip_psum.tile([P, PACK * E // 2], F32, tag="flipped")
+        uv_sums.append(([u1_sums], [v1_sums, v1_last_sums]))
+        for columns in range(2):
+            for i in range(1, PACK):
+                project(i, columns)
         u_rounded = [round_sums(0, 0, nc.scalar.copy)]
         v_rounded = [round_sums(0, 1, nc.scalar.copy)]
         u_mx = quantise(u_rounded[0])

from contextlib import ExitStack
import math

import concourse.mybir as mybir
from concourse.masks import make_identity

BF16 = mybir.dt.bfloat16
F32 = mybir.dt.float32
U32 = mybir.dt.uint32
U8 = mybir.dt.uint8
FP8X4 = mybir.dt.float8_e4m3fn_x4

P = 128
PACK = 4
K_PASS = P * PACK

BATCH = 4
TOKENS = 1024
FEATURES = 1024
E = 128

FEATURE_PASSES = FEATURES // K_PASS
TOKEN_PASSES = TOKENS // K_PASS
TOKEN_TILES = TOKENS // P
WORDS = FEATURES // 2

LOADS = ((0, 0, 2), (0, 2, 2), (1, 0, 2), (1, 2, 1), (1, 3, 1))

IDLE_MATMULS_AT_START = 3
IDLE_COLUMNS_AT_START = 128
IDLE_COLUMNS_BEHIND_A_TILE = 128

FLOPS = 2 * TOKENS * FEATURES * 2 * E + 2 * E * E * TOKENS


def tile_retentionmechanism_pa_s_kernel(tc, y, w_swiglu, out):
    nc = tc.nc

    token_rows = y.flatten_outer_dims().rearrange(
        "(g p t) q -> g p (t q)", g=TOKEN_PASSES, p=P, t=PACK
    )
    weight_tiles = w_swiglu.rearrange("(a p) q -> a p q", p=P)

    with ExitStack() as ctx:
        ctx.enter_context(tc.manual_schedule())
        const = ctx.enter_context(tc.tile_pool(name="const", bufs=1))
        raw_pool = ctx.enter_context(tc.tile_pool(name="raw", bufs=1))
        grouped_pool = ctx.enter_context(tc.tile_pool(name="grouped", bufs=4))
        mx_pool = ctx.enter_context(tc.tile_pool(name="mx", bufs=2 + TOKEN_TILES + 2 * TOKEN_PASSES))
        uv_pool = ctx.enter_context(tc.tile_pool(name="uv", bufs=2 * TOKEN_PASSES))
        flip_psum = ctx.enter_context(tc.psum_pool(name="flip_psum", bufs=4))
        sums_psum = ctx.enter_context(tc.psum_pool(name="sums_psum", bufs=1))

        def load(rows, name):
            raw = raw_pool.tile(list(rows.shape), BF16, name=name)
            nc.sync.dma_start(out=raw[:], in_=rows)
            return [raw[:, i : i + FEATURES] for i in range(0, rows.shape[1], FEATURES)]

        def flip(raw, copy_out, idle):
            words = raw.bitcast(F32)
            flipped = flip_psum.tile([P, WORDS], F32)
            for first in range(0, WORDS, P):
                piece = slice(first, first + P)
                nc.tensor.transpose(flipped[:, piece], words[:, piece], identity[:])
            if idle:
                idle_matmul(IDLE_COLUMNS_BEHIND_A_TILE)
            grouped = grouped_pool.tile([P, FEATURES], BF16, align_bytes=64)
            copy_out(
                out=grouped[:].bitcast(F32).rearrange("p (c r u) -> p c r u", c=FEATURE_PASSES, u=2),
                in_=flipped[:].rearrange("p (c u r) -> p c r u", c=FEATURE_PASSES, u=2),
            )
            return grouped

        def quantise(grouped):
            width = grouped.shape[1] // PACK
            codes = mx_pool.tile([P, width], U32, align_bytes=64)
            scales = mx_pool.tile([P, width], U8, align_bytes=64)
            nc.vector.quantize_mx(out=codes[:].bitcast(FP8X4), scales=scales[:], in_=grouped[:])
            return [
                (codes[:, first : first + P].bitcast(FP8X4), scales[:, first : first + P])
                for first in range(0, width, P)
            ]

        def project(i, columns):
            g, t = divmod(i, PACK)
            for c in range(FEATURE_PASSES):
                token_codes, token_scales = token_mx[i][c]
                weight_codes, weight_scales = weight_mx[columns][c]
                banks = uv_sums[g][columns]
                bank, place = divmod(t, PACK // len(banks))
                nc.tensor.matmul_mx(
                    out=banks[bank][:, place * E : (place + 1) * E],
                    lhsT=token_codes,
                    lhsT_scale=token_scales,
                    rhs=weight_codes,
                    rhs_scale=weight_scales,
                    start=(c == 0),
                    stop=(c == FEATURE_PASSES - 1),
                )

        def idle_matmul(columns):
            nc.tensor.matmul(
                out=unread[:, :columns], lhsT=zeros[:], rhs=zeros[:, :columns], start=True, stop=True
            )

        zeros = const.tile([P, P], F32)
        nc.gpsimd.memset(zeros[:], 0.0)
        unread = sums_psum.tile([P, P], F32, tag="u1_sums")
        for n in range(IDLE_MATMULS_AT_START):
            idle_matmul(IDLE_COLUMNS_AT_START)

        identity = const.tile([P, P], F32)
        make_identity(nc, identity[:])

        weight_raw = [load(weight_tiles[a], "w%d" % a)[0] for a in range(2)]
        token_raw = []
        for g, t, count in LOADS:
            columns = slice(t * FEATURES, (t + count) * FEATURES)
            token_raw += load(token_rows[g, :, columns], "y%d%d" % (g, t))

        weight_grouped = [flip(raw, nc.scalar.copy, True) for raw in weight_raw]
        weight_mx = [quantise(grouped) for grouped in weight_grouped]

        def round_sums(g, columns, copy_out):
            rounded = uv_pool.tile([P, E * PACK], BF16, align_bytes=64)
            by_column = rounded[:].rearrange("p (d t) -> p d t", t=PACK)
            banks = uv_sums[g][columns]
            count = PACK // len(banks)
            for n, bank in enumerate(banks):
                copy_out(
                    out=by_column[:, :, n * count : (n + 1) * count],
                    in_=bank[:].rearrange("p (t d) -> p d t", t=count),
                )
            return rounded

        u0_sums = sums_psum.tile([P, PACK * E], F32)
        v0_sums = sums_psum.tile([P, PACK * E], F32)
        uv_sums = [([u0_sums], [v0_sums])]
        grouped = [flip(token_raw[i], nc.scalar.copy, True) for i in range(2)]
        token_mx = [quantise(grouped[0])]
        grouped += [
            flip(token_raw[2], nc.vector.tensor_copy, False),
            flip(token_raw[3], nc.scalar.copy, False),
        ]
        token_mx += [quantise(grouped[i]) for i in range(1, PACK)]
        project(0, 0)
        project(0, 1)

        grouped = [
            flip(token_raw[4], nc.scalar.copy, False),
            flip(token_raw[5], nc.vector.tensor_copy, False),
            flip(token_raw[6], nc.scalar.copy, False),
            flip(token_raw[7], nc.scalar.copy, False),
        ]
        token_mx += [quantise(tile) for tile in grouped]
        u1_sums = sums_psum.tile([P, PACK * E], F32)
        v1_sums = sums_psum.tile([P, PACK * E // 2], F32)
        v1_last_sums = flip_psum.tile([P, PACK * E // 2], F32, tag="flipped")
        uv_sums.append(([u1_sums], [v1_sums, v1_last_sums]))
        for columns in range(2):
            for i in range(1, PACK):
                project(i, columns)
        u_rounded = [round_sums(0, 0, nc.scalar.copy)]
        v_rounded = [round_sums(0, 1, nc.scalar.copy)]
        u_mx = quantise(u_rounded[0])

        for i, columns in ((4, 0), (5, 0), (6, 0), (4, 1), (5, 1), (7, 0), (6, 1), (7, 1)):
            project(i, columns)
        u_rounded.append(round_sums(1, 0, nc.vector.tensor_copy))
        v_rounded.append(round_sums(1, 1, nc.scalar.copy))
        v_mx = quantise(v_rounded[0])
        u_mx += quantise(u_rounded[1])
        v_mx += quantise(v_rounded[1])

        out_sums = flip_psum.tile([P, E], F32, tag="flipped")
        for g in range(TOKEN_PASSES):
            (u_codes, u_scales), (v_codes, v_scales) = u_mx[g], v_mx[g]
            nc.tensor.matmul_mx(
                out=out_sums[:],
                lhsT=u_codes,
                lhsT_scale=u_scales,
                rhs=v_codes,
                rhs_scale=v_scales,
                start=(g == 0),
                stop=(g == TOKEN_PASSES - 1),
            )
        result = const.tile([P, E], F32)
        nc.vector.tensor_scalar_mul(out=result[:], in0=out_sums[:], scalar1=1.0 / (BATCH * math.sqrt(E)))
        nc.sync.dma_start(out=out, in_=result[:])
